import numpy as np
import ml_dtypes


def mxq(x, axis, fmt="e4m3"):
    dtype, down = {"e4m3": (ml_dtypes.float8_e4m3fn, 7), "e5m2": (ml_dtypes.float8_e5m2, 14)}[fmt]
    v = np.moveaxis(np.asarray(x, np.float32).astype(ml_dtypes.bfloat16).astype(np.float64), axis, -1)
    blocks = v.reshape(v.shape[:-1] + (-1, 32))
    amax = np.abs(blocks).max(-1, keepdims=True)
    byte = np.maximum(np.where(amax > 0, np.frexp(amax)[1] - 1 + 127, 0) - down, 1)
    scale = np.exp2(byte - 127.0)
    codes = (blocks / scale).astype(np.float32).astype(dtype).astype(np.float64)
    return np.moveaxis((codes * scale).reshape(v.shape), -1, axis)


WIDE = False


def mx_kscale(k):
    if not WIDE:
        return np.ones(k)
    levels = np.array([20, -20, 10, -10, 0])
    a = np.random.permutation(np.resize(levels, k // 512 * 4)).reshape(k // 512, 4)
    idx = np.arange(k)
    return np.exp2(a[idx // 512, idx % 128 // 32])


BF16 = ml_dtypes.bfloat16


def bf(x):
    return np.asarray(x, np.float32).astype(BF16)


def f64(x):
    return np.asarray(x).astype(np.float64)


B, S, I, K, O = 512, 16, 256, 2, 512


def setup_inputs():
    u = mx_kscale(O)
    x = np.random.standard_normal((B, S, I))
    a = np.random.standard_normal((1, S, I, K, O)) / np.sqrt(K * I) / u
    a0 = np.random.standard_normal((1, S, I, O)) / np.sqrt(I) / u
    g = np.random.standard_normal((B, S, O)) * np.exp2(np.random.randint(-12, 1, (B, S, 1))) * 8.0 * u
    return {"x": bf(x), "taylor_a_0_1": bf(a), "taylor_a_0": bf(a0), "grad_out": bf(g)}


def reference(x, taylor_a_0_1, taylor_a_0, grad_out):
    g = f64(grad_out).transpose(1, 0, 2)
    a = f64(taylor_a_0_1)[0].transpose(0, 2, 1, 3).reshape(S, K * I, O)
    h = mxq(g, 2, "e5m2") @ mxq(a, 2, "e4m3").transpose(0, 2, 1)
    h = h.reshape(S, B, K, I).transpose(1, 0, 3, 2)
    return h[..., 0] + 2.0 * f64(x) * h[..., 1]

@@ -1,0 +1,226 @@
+from contextlib import ExitStack
+
+import concourse.mybir as mybir
+from concourse.masks import make_identity
+
+F32 = mybir.dt.float32
+BF16 = mybir.dt.bfloat16
+U32 = mybir.dt.uint32
+U8 = mybir.dt.uint8
+E4M3_X4 = mybir.dt.float8_e4m3fn_x4
+E5M2_X4 = mybir.dt.float8_e5m2_x4
+MULT = mybir.AluOpType.mult
+ADD = mybir.AluOpType.add
+
+B, S, I, K, O = 512, 16, 256, 2, 512
+
+P = 128
+PACK = 4
+HALVES = 2
+ROW_WORDS = O // 2
+B_TILES = B // P
+I_PER_Q = I // P
+COLS = K * I
+PAIR = 2
+PAIRS = S // PAIR
+STEPS = B_TILES * PAIRS
+G_POSITIONS = 8
+G_PAIRS = G_POSITIONS // PAIR
+OUT_POSITIONS = 4
+OUT_PAIRS = OUT_POSITIONS // PAIR
+BANK_BLOCKS = 4
+
+FLOPS = 2 * B * S * K * I * O
+BYTES = 2 * B * S * I + 2 * S * I * K * O + 2 * B * S * O + 4 * B * S * I
+
+
+def tile_modelsingle_t_kernel(tc, x, taylor_a_0_1, taylor_a_0, grad_out, out):
+    nc = tc.nc
+    a_rows = taylor_a_0_1.rearrange("one s (q ih) p o -> q (one s) (ih p o)", ih=I_PER_Q)
+
+    with ExitStack() as stack:
+        keep = stack.enter_context(tc.tile_pool(name="keep", bufs=1))
+        a_pool = stack.enter_context(tc.tile_pool(name="a_pool", bufs=4))
+        g_pool = stack.enter_context(tc.tile_pool(name="g_pool", bufs=B_TILES * S // G_POSITIONS))
+        x_pool = stack.enter_context(tc.tile_pool(name="x_pool", bufs=B_TILES))
+        grouped_pool = stack.enter_context(tc.tile_pool(name="grouped_pool", bufs=3))
+        codes_pool = stack.enter_context(tc.tile_pool(name="codes_pool", bufs=3))
+        work_pool = stack.enter_context(tc.tile_pool(name="work_pool", bufs=6))
+        out_pool = stack.enter_context(tc.tile_pool(name="out_pool", bufs=4))
+        flipped_psum = stack.enter_context(tc.psum_pool(name="flipped_psum", bufs=4))
+        acc_psum = stack.enter_context(tc.psum_pool(name="acc_psum", bufs=4))
+        stack.enter_context(tc.manual_schedule())
+
+        identity = keep.tile([P, P], F32)
+        make_identity(nc, identity[:])
+        a_codes = keep.tile([P, S * COLS], U32, align_bytes=64)
+        a_scales = keep.tile([P, S * COLS], U8, align_bytes=64)
+
+        a_raw_of = {}
+        g_raw_of = {}
+        x_of = {}
+        a_grouped_of = {}
+        g_grouped_of = {}
+        g_mx_of = {}
+        second_of = {}
+        out_of = {}
+
+        def load(step):
+            bt, pair = divmod(step, PAIRS)
+            b_rows = slice(bt * P, (bt + 1) * P)
+            if bt == 0:
+                a_raw = a_pool.tile([P, PAIR * I_PER_Q * K * O], BF16)
+                nc.sync.dma_start(
+                    out=a_raw[:].rearrange("q (s r) -> q s r", s=PAIR),
+                    in_=a_rows[:, pair * PAIR : (pair + 1) * PAIR, :],
+                )
+                a_raw_of[pair] = a_raw
+            if pair % G_PAIRS == 0:
+                first = pair * PAIR
+                g_raw = g_pool.tile([P, G_POSITIONS * O], BF16)
+                nc.sync.dma_start(
+                    out=g_raw[:],
+                    in_=grad_out[b_rows, first : first + G_POSITIONS, :].rearrange("b s o -> b (s o)"),
+                )
+                g_raw_of[(bt, pair // G_PAIRS)] = g_raw
+            if pair == 0:
+                x_sb = x_pool.tile([P, S * I], BF16)
+                nc.sync.dma_start(out=x_sb[:], in_=x[b_rows, :, :].rearrange("b s i -> b (s i)"))
+                x_of[bt] = x_sb
+
+        def flip_coefficients(pair):
+            a_words = a_raw_of[pair][:].bitcast(F32)
+            a_grouped = grouped_pool.tile([P, PAIR * COLS * PACK], BF16, align_bytes=64)
+            a_grouped_words = a_grouped[:].bitcast(F32)
+            for j in range(PAIR):
+                for p in range(K):
+                    a_flipped = flipped_psum.tile([P, BANK_BLOCKS, P], F32, tag="flipped")
+                    for ih in range(I_PER_Q):
+                        for u in range(HALVES):
+                            first = (((j * I_PER_Q + ih) * K + p) * HALVES + u) * P
+                            nc.tensor.transpose(
+                                a_flipped[:, ih * HALVES + u, :], a_words[:, first : first + P], identity[:]
+                            )
+                    first = (j * K + p) * I * HALVES
+                    nc.scalar.copy(
+                        out=a_grouped_words[:, first : first + I * HALVES].rearrange(
+                            "w (q ih u) -> w q ih u", ih=I_PER_Q, u=HALVES
+                        ),
+                        in_=a_flipped[:].rearrange("w (ih u) q -> w q ih u", u=HALVES),
+                    )
+            a_grouped_of[pair] = a_grouped
+
+        def flip_gradient(step):
+            bt, pair = divmod(step, PAIRS)
+            g_words = g_raw_of[(bt, pair // G_PAIRS)][:].bitcast(F32)
+            g_flipped = flipped_psum.tile([P, BANK_BLOCKS, P], F32, tag="flipped")
+            for j in range(PAIR):
+                for u in range(HALVES):
+                    first = (((pair % G_PAIRS) * PAIR + j) * HALVES + u) * P
+                    nc.tensor.transpose(
+                        g_flipped[:, j * HALVES + u, :], g_words[:, first : first + P], identity[:]
+                    )
+            g_grouped = grouped_pool.tile([P, PAIR * P * PACK], BF16, align_bytes=64)
+            nc.scalar.copy(
+                out=g_grouped[:].bitcast(F32).rearrange("w (j b u) -> w j b u", j=PAIR, u=HALVES),
+                in_=g_flipped[:].rearrange("w (j u) b -> w j b u", u=HALVES),
+            )
+            g_grouped_of[step] = g_grouped
+
+        def flip(step):
+            if step < PAIRS:
+                flip_coefficients(step)
+            flip_gradient(step)
+
+        def quantise(step):
+            if step < PAIRS:
+                cols = slice(step * PAIR * COLS, (step + 1) * PAIR * COLS)
+                nc.vector.quantize_mx(
+                    out=a_codes[:, cols].bitcast(E4M3_X4), scales=a_scales[:, cols], in_=a_grouped_of[step][:]
+                )
+            g_codes = codes_pool.tile([P, PAIR * P], U32, align_bytes=64)
+            g_scales = codes_pool.tile([P, PAIR * P], U8, align_bytes=64)
+            nc.vector.quantize_mx(
+                out=g_codes[:].bitcast(E5M2_X4), scales=g_scales[:], in_=g_grouped_of[step][:]
+            )
+            g_mx_of[step] = (g_codes, g_scales)
+
+        def multiply(step):
+            bt, pair = divmod(step, PAIRS)
+            g_codes, g_scales = g_mx_of[step]
+            if pair % OUT_PAIRS == 0:
+                out_sb = out_pool.tile([P, OUT_POSITIONS * I], F32)
+                out_of[(bt, pair // OUT_PAIRS)] = out_sb
+            out_sb = out_of[(bt, pair // OUT_PAIRS)]
+            accs = []
+            for j in range(PAIR):
+                s = pair * PAIR + j
+                acc = acc_psum.tile([P, COLS], F32)
+                nc.tensor.matmul_mx(
+                    out=acc[:],
+                    lhsT=g_codes[:, j * P : (j + 1) * P].bitcast(E5M2_X4),
+                    lhsT_scale=g_scales[:, j * P : (j + 1) * P],
+                    rhs=a_codes[:, s * COLS : (s + 1) * COLS].bitcast(E4M3_X4),
+                    rhs_scale=a_scales[:, s * COLS : (s + 1) * COLS],
+                    start=True,
+                    stop=True,
+                )
+                accs.append(acc)
+            twice_x_h1s = []
+            for j in range(PAIR):
+                s = pair * PAIR + j
+                twice_x_h1 = work_pool.tile([P, I], F32)
+                nc.vector.scalar_tensor_tensor(
+                    out=twice_x_h1[:],
+                    in0=accs[j][:, I : 2 * I],
+                    scalar=2.0,
+                    in1=x_of[bt][:, s * I : (s + 1) * I],
+                    op0=MULT,
+                    op1=MULT,
+                )
+                twice_x_h1s.append(twice_x_h1)
+            first_place = (pair % OUT_PAIRS) * PAIR * I
+            nc.vector.tensor_tensor(
+                out=out_sb[:, first_place : first_place + I],
+                in0=twice_x_h1s[0][:],
+                in1=accs[0][:, 0:I],
+                op=ADD,
+            )
+            second_of[step] = (accs[1], twice_x_h1s[1])
+
+        def finish(step):
+            bt, pair = divmod(step, PAIRS)
+            acc, twice_x_h1 = second_of[step]
+            out_sb = out_of[(bt, pair // OUT_PAIRS)]
+            second_place = ((pair % OUT_PAIRS) * PAIR + 1) * I
+            nc.scalar.copy(out=out_sb[:, second_place : second_place + I], in_=acc[:, 0:I])
+            nc.gpsimd.tensor_tensor(
+                out=out_sb[:, second_place : second_place + I],
+                in0=out_sb[:, second_place : second_place + I],
+                in1=twice_x_h1[:],
+                op=ADD,
+            )
+
+        def store(step):
+            bt, pair = divmod(step, PAIRS)
+            if pair % OUT_PAIRS == OUT_PAIRS - 1:
+                first = (pair + 1) * PAIR - OUT_POSITIONS
+                nc.scalar.dma_start(
+                    out=out[bt * P : (bt + 1) * P, first : first + OUT_POSITIONS, :].rearrange("b s i -> b (s i)"),
+                    in_=out_of[(bt, pair // OUT_PAIRS)][:],
+                )
+
+        steps = range(STEPS)
+        for n in range(-3, STEPS + 2):
+            if n + 3 in steps:
+                load(n + 3)
+            if n + 2 in steps:
+                flip(n + 2)
+            if n + 1 in steps:
+                quantise(n + 1)
+            if n in steps:
+                multiply(n)
+            if n - 1 in steps:
+                finish(n - 1)
+            if n - 2 in steps:
+                store(n - 2)

@@ -17,18 +17,18 @@ B, S, I, K, O = 512, 16, 256, 2, 512
 P = 128
 PACK = 4
 HALVES = 2
-ROW_WORDS = O // 2
 B_TILES = B // P
 I_PER_Q = I // P
 COLS = K * I
 PAIR = 2
-PAIRS = S // PAIR
-STEPS = B_TILES * PAIRS
-G_POSITIONS = 8
-G_PAIRS = G_POSITIONS // PAIR
-OUT_POSITIONS = 4
-OUT_PAIRS = OUT_POSITIONS // PAIR
-BANK_BLOCKS = 4
+GROUP = 4
+PAIRS = GROUP // PAIR
+GROUP_STEPS = B_TILES * PAIRS
+STEPS = (S // GROUP) * GROUP_STEPS
+BLOCKS = S * K
+PAIR_BLOCKS = PAIR * K
+BLOCK_LEAD = GROUP * K
+BANK_SQUARES = 4
 
 FLOPS = 2 * B * S * K * I * O
 BYTES = 2 * B * S * I + 2 * S * I * K * O + 2 * B * S * O + 4 * B * S * I
@@ -41,8 +41,7 @@ def tile_modelsingle_t_kernel(tc, x, taylor_a_0_1, taylor_a_0, grad_out, out):
     with ExitStack() as stack:
         keep = stack.enter_context(tc.tile_pool(name="keep", bufs=1))
         a_pool = stack.enter_context(tc.tile_pool(name="a_pool", bufs=4))
-        g_pool = stack.enter_context(tc.tile_pool(name="g_pool", bufs=B_TILES * S // G_POSITIONS))
-        x_pool = stack.enter_context(tc.tile_pool(name="x_pool", bufs=B_TILES))
+        gx_pool = stack.enter_context(tc.tile_pool(name="gx_pool", bufs=STEPS // PAIRS))
         grouped_pool = stack.enter_context(tc.tile_pool(name="grouped_pool", bufs=3))
         codes_pool = stack.enter_context(tc.tile_pool(name="codes_pool", bufs=3))
         work_pool = stack.enter_context(tc.tile_pool(name="work_pool", bufs=6))
@@ -65,58 +64,56 @@ def tile_modelsingle_t_kernel(tc, x, taylor_a_0_1, taylor_a_0, grad_out, out):
         second_of = {}
         out_of = {}
 
+        def where(step):
+            group, rest = divmod(step, GROUP_STEPS)
+            bt = rest // PAIRS
+            return slice(bt * P, (bt + 1) * P), group * GROUP
+
         def load(step):
-            bt, pair = divmod(step, PAIRS)
-            b_rows = slice(bt * P, (bt + 1) * P)
-            if bt == 0:
+            block = step + BLOCK_LEAD
+            if step in range(STEPS) and step % PAIRS == 0:
+                b_rows, first = where(step)
+                g_raw = gx_pool.tile([P, GROUP * O], BF16)
+                nc.sync.dma_start(
+                    out=g_raw[:], in_=grad_out[b_rows, first : first + GROUP, :].rearrange("b s o -> b (s o)")
+                )
+                g_raw_of[step // PAIRS] = g_raw
+                x_sb = gx_pool.tile([P, GROUP * I], BF16)
+                nc.sync.dma_start(
+                    out=x_sb[:], in_=x[b_rows, first : first + GROUP, :].rearrange("b s i -> b (s i)")
+                )
+                x_of[step // PAIRS] = x_sb
+            if block in range(BLOCKS) and block % PAIR_BLOCKS == 0:
+                first = block // K
                 a_raw = a_pool.tile([P, PAIR * I_PER_Q * K * O], BF16)
                 nc.sync.dma_start(
-                    out=a_raw[:].rearrange("q (s r) -> q s r", s=PAIR),
-                    in_=a_rows[:, pair * PAIR : (pair + 1) * PAIR, :],
+                    out=a_raw[:].rearrange("q (s r) -> q s r", s=PAIR), in_=a_rows[:, first : first + PAIR, :]
                 )
-                a_raw_of[pair] = a_raw
-            if pair % G_PAIRS == 0:
-                first = pair * PAIR
-                g_raw = g_pool.tile([P, G_POSITIONS * O], BF16)
-                nc.sync.dma_start(
-                    out=g_raw[:],
-                    in_=grad_out[b_rows, first : first + G_POSITIONS, :].rearrange("b s o -> b (s o)"),
-                )
-                g_raw_of[(bt, pair // G_PAIRS)] = g_raw
-            if pair == 0:
-                x_sb = x_pool.tile([P, S * I], BF16)
-                nc.sync.dma_start(out=x_sb[:], in_=x[b_rows, :, :].rearrange("b s i -> b (s i)"))
-                x_of[bt] = x_sb
+                a_raw_of[block // PAIR_BLOCKS] = a_raw
 
-        def flip_coefficients(pair):
-            a_words = a_raw_of[pair][:].bitcast(F32)
-            a_grouped = grouped_pool.tile([P, PAIR * COLS * PACK], BF16, align_bytes=64)
-            a_grouped_words = a_grouped[:].bitcast(F32)
-            for j in range(PAIR):
-                for p in range(K):
-                    a_flipped = flipped_psum.tile([P, BANK_BLOCKS, P], F32, tag="flipped")
-                    for ih in range(I_PER_Q):
-                        for u in range(HALVES):
-                            first = (((j * I_PER_Q + ih) * K + p) * HALVES + u) * P
-                            nc.tensor.transpose(
-                                a_flipped[:, ih * HALVES + u, :], a_words[:, first : first + P], identity[:]
-                            )
-                    first = (j * K + p) * I * HALVES
-                    nc.scalar.copy(
-                        out=a_grouped_words[:, first : first + I * HALVES].rearrange(
-                            "w (q ih u) -> w q ih u", ih=I_PER_Q, u=HALVES
-                        ),
-                        in_=a_flipped[:].rearrange("w (ih u) q -> w q ih u", u=HALVES),
+        def flip_coefficients(block):
+            j, p = divmod(block % PAIR_BLOCKS, K)
+            a_words = a_raw_of[block // PAIR_BLOCKS][:].bitcast(F32)
+            a_flipped = flipped_psum.tile([P, BANK_SQUARES, P], F32, tag="flipped")
+            for ih in range(I_PER_Q):
+                for u in range(HALVES):
+                    first = (((j * I_PER_Q + ih) * K + p) * HALVES + u) * P
+                    nc.tensor.transpose(
+                        a_flipped[:, ih * HALVES + u, :], a_words[:, first : first + P], identity[:]
                     )
-            a_grouped_of[pair] = a_grouped
+            a_grouped = grouped_pool.tile([P, I * PACK], BF16, align_bytes=64)
+            nc.scalar.copy(
+                out=a_grouped[:].bitcast(F32).rearrange("w (q ih u) -> w q ih u", ih=I_PER_Q, u=HALVES),
+                in_=a_flipped[:].rearrange("w (ih u) q -> w q ih u", u=HALVES),
+            )
+            a_grouped_of[block] = a_grouped
 
         def flip_gradient(step):
-            bt, pair = divmod(step, PAIRS)
-            g_words = g_raw_of[(bt, pair // G_PAIRS)][:].bitcast(F32)
-            g_flipped = flipped_psum.tile([P, BANK_BLOCKS, P], F32, tag="flipped")
+            g_words = g_raw_of[step // PAIRS][:].bitcast(F32)
+            g_flipped = flipped_psum.tile([P, BANK_SQUARES, P], F32, tag="flipped")
             for j in range(PAIR):
                 for u in range(HALVES):
-                    first = (((pair % G_PAIRS) * PAIR + j) * HALVES + u) * P
+                    first = (((step % PAIRS) * PAIR + j) * HALVES + u) * P
                     nc.tensor.transpose(
                         g_flipped[:, j * HALVES + u, :], g_words[:, first : first + P], identity[:]
                     )
@@ -128,33 +125,38 @@ def tile_modelsingle_t_kernel(tc, x, taylor_a_0_1, taylor_a_0, grad_out, out):
             g_grouped_of[step] = g_grouped
 
         def flip(step):
-            if step < PAIRS:
-                flip_coefficients(step)
-            flip_gradient(step)
+            if step + BLOCK_LEAD in range(BLOCKS):
+                flip_coefficients(step + BLOCK_LEAD)
+            if step in range(STEPS):
+                flip_gradient(step)
 
         def quantise(step):
-            if step < PAIRS:
-                cols = slice(step * PAIR * COLS, (step + 1) * PAIR * COLS)
+            block = step + BLOCK_LEAD
+            if block in range(BLOCKS):
+                cols = slice(block * I, (block + 1) * I)
                 nc.vector.quantize_mx(
-                    out=a_codes[:, cols].bitcast(E4M3_X4), scales=a_scales[:, cols], in_=a_grouped_of[step][:]
+                    out=a_codes[:, cols].bitcast(E4M3_X4), scales=a_scales[:, cols], in_=a_grouped_of[block][:]
                 )
-            g_codes = codes_pool.tile([P, PAIR * P], U32, align_bytes=64)
-            g_scales = codes_pool.tile([P, PAIR * P], U8, align_bytes=64)
-            nc.vector.quantize_mx(
-                out=g_codes[:].bitcast(E5M2_X4), scales=g_scales[:], in_=g_grouped_of[step][:]
-            )
-            g_mx_of[step] = (g_codes, g_scales)
+            if step in range(STEPS):
+                g_codes = codes_pool.tile([P, PAIR * P], U32, align_bytes=64)
+                g_scales = codes_pool.tile([P, PAIR * P], U8, align_bytes=64)
+                nc.vector.quantize_mx(
+                    out=g_codes[:].bitcast(E5M2_X4), scales=g_scales[:], in_=g_grouped_of[step][:]
+                )
+                g_mx_of[step] = (g_codes, g_scales)
 
         def multiply(step):
-            bt, pair = divmod(step, PAIRS)
+            if step not in range(STEPS):
+                return
+            first = where(step)[1]
             g_codes, g_scales = g_mx_of[step]
-            if pair % OUT_PAIRS == 0:
-                out_sb = out_pool.tile([P, OUT_POSITIONS * I], F32)
-                out_of[(bt, pair // OUT_PAIRS)] = out_sb
-            out_sb = out_of[(bt, pair // OUT_PAIRS)]
+            if step % PAIRS == 0:
+                out_sb = out_pool.tile([P, GROUP * I], F32)
+                out_of[step // PAIRS] = out_sb
+            out_sb = out_of[step // PAIRS]
             accs = []
             for j in range(PAIR):
-                s = pair * PAIR + j
+                s = first + (step % PAIRS) * PAIR + j
                 acc = acc_psum.tile([P, COLS], F32)
                 nc.tensor.matmul_mx(
                     out=acc[:],
@@ -168,59 +170,44 @@ def tile_modelsingle_t_kernel(tc, x, taylor_a_0_1, taylor_a_0, grad_out, out):
                 accs.append(acc)
             twice_x_h1s = []
             for j in range(PAIR):
-                s = pair * PAIR + j
+                place = ((step % PAIRS) * PAIR + j) * I
                 twice_x_h1 = work_pool.tile([P, I], F32)
                 nc.vector.scalar_tensor_tensor(
                     out=twice_x_h1[:],
                     in0=accs[j][:, I : 2 * I],
                     scalar=2.0,
-                    in1=x_of[bt][:, s * I : (s + 1) * I],
+                    in1=x_of[step // PAIRS][:, place : place + I],
                     op0=MULT,
                     op1=MULT,
                 )
                 twice_x_h1s.append(twice_x_h1)
-            first_place = (pair % OUT_PAIRS) * PAIR * I
+            place = (step % PAIRS) * PAIR * I
             nc.vector.tensor_tensor(
-                out=out_sb[:, first_place : first_place + I],
-                in0=twice_x_h1s[0][:],
-                in1=accs[0][:, 0:I],
-                op=ADD,
+                out=out_sb[:, place : place + I], in0=twice_x_h1s[0][:], in1=accs[0][:, 0:I], op=ADD
             )
             second_of[step] = (accs[1], twice_x_h1s[1])
 
         def finish(step):
-            bt, pair = divmod(step, PAIRS)
+            if step not in range(STEPS):
+                return
             acc, twice_x_h1 = second_of[step]
-            out_sb = out_of[(bt, pair // OUT_PAIRS)]
-            second_place = ((pair % OUT_PAIRS) * PAIR + 1) * I
-            nc.scalar.copy(out=out_sb[:, second_place : second_place + I], in_=acc[:, 0:I])
-            nc.gpsimd.tensor_tensor(
-                out=out_sb[:, second_place : second_place + I],
-                in0=out_sb[:, second_place : second_place + I],
-                in1=twice_x_h1[:],
-                op=ADD,
-            )
+            place = ((step % PAIRS) * PAIR + 1) * I
+            result = out_of[step // PAIRS][:, place : place + I]
+            nc.scalar.copy(out=result, in_=acc[:, 0:I])
+            nc.gpsimd.tensor_tensor(out=result, in0=result, in1=twice_x_h1[:], op=ADD)
 
         def store(step):
-            bt, pair = divmod(step, PAIRS)
-            if pair % OUT_PAIRS == OUT_PAIRS - 1:
-                first = (pair + 1) * PAIR - OUT_POSITIONS
+            if step in range(STEPS) and step % PAIRS == PAIRS - 1:
+                b_rows, first = where(step)
                 nc.scalar.dma_start(
-                    out=out[bt * P : (bt + 1) * P, first : first + OUT_POSITIONS, :].rearrange("b s i -> b (s i)"),
-                    in_=out_of[(bt, pair // OUT_PAIRS)][:],
+                    out=out[b_rows, first : first + GROUP, :].rearrange("b s i -> b (s i)"),
+                    in_=out_of[step // PAIRS][:],
                 )
 
-        steps = range(STEPS)
-        for n in range(-3, STEPS + 2):
-            if n + 3 in steps:
-                load(n + 3)
-            if n + 2 in steps:
-                flip(n + 2)
-            if n + 1 in steps:
-                quantise(n + 1)
-            if n in steps:
-                multiply(n)
-            if n - 1 in steps:
-                finish(n - 1)
-            if n - 2 in steps:
-                store(n - 2)
+        for n in range(-BLOCK_LEAD - 4, STEPS + 2):
+            load(n + 4)
+            finish(n - 1)
+            flip(n + 2)
+            quantise(n + 1)
+            multiply(n)
+            store(n - 2)

@@ -29,6 +29,7 @@ BLOCKS = S * K
 PAIR_BLOCKS = PAIR * K
 BLOCK_LEAD = GROUP * K
 BANK_SQUARES = 4
+STORE_LAG = 12
 
 FLOPS = 2 * B * S * K * I * O
 BYTES = 2 * B * S * I + 2 * S * I * K * O + 2 * B * S * O + 4 * B * S * I
@@ -45,7 +46,7 @@ def tile_modelsingle_t_kernel(tc, x, taylor_a_0_1, taylor_a_0, grad_out, out):
         grouped_pool = stack.enter_context(tc.tile_pool(name="grouped_pool", bufs=3))
         codes_pool = stack.enter_context(tc.tile_pool(name="codes_pool", bufs=3))
         work_pool = stack.enter_context(tc.tile_pool(name="work_pool", bufs=6))
-        out_pool = stack.enter_context(tc.tile_pool(name="out_pool", bufs=4))
+        out_pool = stack.enter_context(tc.tile_pool(name="out_pool", bufs=STORE_LAG // PAIRS + 4))
         flipped_psum = stack.enter_context(tc.psum_pool(name="flipped_psum", bufs=4))
         acc_psum = stack.enter_context(tc.psum_pool(name="acc_psum", bufs=4))
         stack.enter_context(tc.manual_schedule())
@@ -199,15 +200,15 @@ def tile_modelsingle_t_kernel(tc, x, taylor_a_0_1, taylor_a_0, grad_out, out):
         def store(step):
             if step in range(STEPS) and step % PAIRS == PAIRS - 1:
                 b_rows, first = where(step)
-                nc.scalar.dma_start(
+                nc.sync.dma_start(
                     out=out[b_rows, first : first + GROUP, :].rearrange("b s i -> b (s i)"),
                     in_=out_of[step // PAIRS][:],
                 )
 
-        for n in range(-BLOCK_LEAD - 4, STEPS + 2):
+        for n in range(-BLOCK_LEAD - 4, STEPS + STORE_LAG):
             load(n + 4)
             finish(n - 1)
             flip(n + 2)
             quantise(n + 1)
             multiply(n)
-            store(n - 2)
+            store(n - STORE_LAG)

@@ -21,13 +21,14 @@ B_TILES = B // P
 I_PER_Q = I // P
 COLS = K * I
 PAIR = 2
-GROUP = 4
+GROUP = 8
 PAIRS = GROUP // PAIR
 GROUP_STEPS = B_TILES * PAIRS
 STEPS = (S // GROUP) * GROUP_STEPS
 BLOCKS = S * K
 PAIR_BLOCKS = PAIR * K
-BLOCK_LEAD = GROUP * K
+BLOCK_LEAD = PAIRS * PAIR_BLOCKS - 1 - (PAIRS - 1) + 1
+SHARED = 4
 BANK_SQUARES = 4
 STORE_LAG = 12
 
@@ -42,11 +43,11 @@ def tile_modelsingle_t_kernel(tc, x, taylor_a_0_1, taylor_a_0, grad_out, out):
     with ExitStack() as stack:
         keep = stack.enter_context(tc.tile_pool(name="keep", bufs=1))
         a_pool = stack.enter_context(tc.tile_pool(name="a_pool", bufs=4))
-        gx_pool = stack.enter_context(tc.tile_pool(name="gx_pool", bufs=STEPS // PAIRS))
+        gx_pool = stack.enter_context(tc.tile_pool(name="gx_pool", bufs=4))
         grouped_pool = stack.enter_context(tc.tile_pool(name="grouped_pool", bufs=3))
         codes_pool = stack.enter_context(tc.tile_pool(name="codes_pool", bufs=3))
-        work_pool = stack.enter_context(tc.tile_pool(name="work_pool", bufs=6))
-        out_pool = stack.enter_context(tc.tile_pool(name="out_pool", bufs=STORE_LAG // PAIRS + 4))
+        work_pool = stack.enter_context(tc.tile_pool(name="work_pool", bufs=8))
+        out_pool = stack.enter_context(tc.tile_pool(name="out_pool", bufs=STORE_LAG // PAIRS + 3))
         flipped_psum = stack.enter_context(tc.psum_pool(name="flipped_psum", bufs=4))
         acc_psum = stack.enter_context(tc.psum_pool(name="acc_psum", bufs=4))
         stack.enter_context(tc.manual_schedule())
@@ -64,6 +65,7 @@ def tile_modelsingle_t_kernel(tc, x, taylor_a_0_1, taylor_a_0, grad_out, out):
         g_mx_of = {}
         second_of = {}
         out_of = {}
+        left_of = {}
 
         def where(step):
             group, rest = divmod(step, GROUP_STEPS)
@@ -183,23 +185,36 @@ def tile_modelsingle_t_kernel(tc, x, taylor_a_0_1, taylor_a_0, grad_out, out):
                 )
                 twice_x_h1s.append(twice_x_h1)
             place = (step % PAIRS) * PAIR * I
-            nc.vector.tensor_tensor(
-                out=out_sb[:, place : place + I], in0=twice_x_h1s[0][:], in1=accs[0][:, 0:I], op=ADD
-            )
-            second_of[step] = (accs[1], twice_x_h1s[1])
+            if step % SHARED == SHARED - 1:
+                left_of[step] = [0, 1]
+            else:
+                left_of[step] = [1]
+                nc.vector.tensor_tensor(
+                    out=out_sb[:, place : place + I], in0=twice_x_h1s[0][:], in1=accs[0][:, 0:I], op=ADD
+                )
+            second_of[step] = (accs, twice_x_h1s)
 
         def finish(step):
             if step not in range(STEPS):
                 return
-            acc, twice_x_h1 = second_of[step]
-            place = ((step % PAIRS) * PAIR + 1) * I
-            result = out_of[step // PAIRS][:, place : place + I]
-            nc.scalar.copy(out=result, in_=acc[:, 0:I])
-            nc.gpsimd.tensor_tensor(out=result, in0=result, in1=twice_x_h1[:], op=ADD)
+            accs, twice_x_h1s = second_of[step]
+            for j in left_of[step]:
+                place = ((step % PAIRS) * PAIR + j) * I
+                result = out_of[step // PAIRS][:, place : place + I]
+                nc.scalar.copy(out=result, in_=accs[j][:, 0:I])
+                nc.gpsimd.tensor_tensor(out=result, in0=result, in1=twice_x_h1s[j][:], op=ADD)
 
         def store(step):
-            if step in range(STEPS) and step % PAIRS == PAIRS - 1:
-                b_rows, first = where(step)
+            if step not in range(STEPS):
+                return
+            b_rows, first = where(step)
+            if step >= STEPS - PAIRS:
+                k = step % PAIRS
+                nc.sync.dma_start(
+                    out=out[b_rows, first + k * PAIR : first + (k + 1) * PAIR, :].rearrange("b s i -> b (s i)"),
+                    in_=out_of[step // PAIRS][:, k * PAIR * I : (k + 1) * PAIR * I],
+                )
+            elif step % PAIRS == PAIRS - 1:
                 nc.sync.dma_start(
                     out=out[b_rows, first : first + GROUP, :].rearrange("b s i -> b (s i)"),
                     in_=out_of[step // PAIRS][:],

@@ -28,7 +28,7 @@ STEPS = (S // GROUP) * GROUP_STEPS
 BLOCKS = S * K
 PAIR_BLOCKS = PAIR * K
 BLOCK_LEAD = PAIRS * PAIR_BLOCKS - 1 - (PAIRS - 1) + 1
-SHARED = 4
+TAIL_STEPS = 2
 BANK_SQUARES = 4
 STORE_LAG = 12
 
@@ -185,13 +185,15 @@ def tile_modelsingle_t_kernel(tc, x, taylor_a_0_1, taylor_a_0, grad_out, out):
                 )
                 twice_x_h1s.append(twice_x_h1)
             place = (step % PAIRS) * PAIR * I
-            if step % SHARED == SHARED - 1:
-                left_of[step] = [0, 1]
-            else:
-                left_of[step] = [1]
-                nc.vector.tensor_tensor(
-                    out=out_sb[:, place : place + I], in0=twice_x_h1s[0][:], in1=accs[0][:, 0:I], op=ADD
-                )
+            left_of[step] = [] if step >= STEPS - TAIL_STEPS else [1]
+            for j in range(PAIR):
+                if j not in left_of[step]:
+                    nc.vector.tensor_tensor(
+                        out=out_sb[:, place + j * I : place + (j + 1) * I],
+                        in0=twice_x_h1s[j][:],
+                        in1=accs[j][:, 0:I],
+                        op=ADD,
+                    )
             second_of[step] = (accs, twice_x_h1s)
 
         def finish(step):

@@ -18,7 +18,7 @@ P = 128
 PACK = 4
 HALVES = 2
 B_TILES = B // P
-I_PER_Q = I // P
+I_PER_Q = 2 * I // P
 COLS = K * I
 PAIR = 2
 GROUP = 8
@@ -38,7 +38,7 @@ BYTES = 2 * B * S * I + 2 * S * I * K * O + 2 * B * S * O + 4 * B * S * I
 
 def tile_modelsingle_t_kernel(tc, x, taylor_a_0_1, taylor_a_0, grad_out, out):
     nc = tc.nc
-    a_rows = taylor_a_0_1.rearrange("one s (q ih) p o -> q (one s) (ih p o)", ih=I_PER_Q)
+    a_rows = taylor_a_0_1.rearrange("one (m sj) (q ih) p o -> (sj q) (one m) (ih p o)", sj=PAIR, ih=I_PER_Q)
 
     with ExitStack() as stack:
         keep = stack.enter_context(tc.tile_pool(name="keep", bufs=1))
@@ -87,29 +87,31 @@ def tile_modelsingle_t_kernel(tc, x, taylor_a_0_1, taylor_a_0, grad_out, out):
                 )
                 x_of[step // PAIRS] = x_sb
             if block in range(BLOCKS) and block % PAIR_BLOCKS == 0:
-                first = block // K
-                a_raw = a_pool.tile([P, PAIR * I_PER_Q * K * O], BF16)
-                nc.sync.dma_start(
-                    out=a_raw[:].rearrange("q (s r) -> q s r", s=PAIR), in_=a_rows[:, first : first + PAIR, :]
-                )
-                a_raw_of[block // PAIR_BLOCKS] = a_raw
+                m = block // PAIR_BLOCKS
+                a_raw = a_pool.tile([P, I_PER_Q * K * O], BF16)
+                nc.sync.dma_start(out=a_raw[:], in_=a_rows[:, m : m + 1, :].rearrange("c m r -> c (m r)"))
+                a_raw_of[m] = a_raw
 
         def flip_coefficients(block):
-            j, p = divmod(block % PAIR_BLOCKS, K)
+            p, h = divmod(block % PAIR_BLOCKS, 2)
             a_words = a_raw_of[block // PAIR_BLOCKS][:].bitcast(F32)
             a_flipped = flipped_psum.tile([P, BANK_SQUARES, P], F32, tag="flipped")
-            for ih in range(I_PER_Q):
+            for il in range(2):
                 for u in range(HALVES):
-                    first = (((j * I_PER_Q + ih) * K + p) * HALVES + u) * P
+                    first = (((2 * h + il) * K + p) * HALVES + u) * P
                     nc.tensor.transpose(
-                        a_flipped[:, ih * HALVES + u, :], a_words[:, first : first + P], identity[:]
+                        a_flipped[:, il * HALVES + u, :], a_words[:, first : first + P], identity[:]
                     )
-            a_grouped = grouped_pool.tile([P, I * PACK], BF16, align_bytes=64)
+            if h == 0:
+                a_grouped = grouped_pool.tile([P, PAIR * I * PACK], BF16, align_bytes=64)
+                a_grouped_of[block // 2] = a_grouped
+            a_grouped = a_grouped_of[block // 2]
             nc.scalar.copy(
-                out=a_grouped[:].bitcast(F32).rearrange("w (q ih u) -> w q ih u", ih=I_PER_Q, u=HALVES),
-                in_=a_flipped[:].rearrange("w (ih u) q -> w q ih u", u=HALVES),
+                out=a_grouped[:].bitcast(F32).rearrange("w (c r) -> w c r", r=2 * BANK_SQUARES)[
+                    :, :, h * BANK_SQUARES : (h + 1) * BANK_SQUARES
+                ],
+                in_=a_flipped[:].rearrange("w r c -> w c r"),
             )
-            a_grouped_of[block] = a_grouped
 
         def flip_gradient(step):
             g_words = g_raw_of[step // PAIRS][:].bitcast(F32)
@@ -134,11 +136,16 @@ def tile_modelsingle_t_kernel(tc, x, taylor_a_0_1, taylor_a_0, grad_out, out):
                 flip_gradient(step)
 
         def quantise(step):
-            block = step + BLOCK_LEAD
-            if block in range(BLOCKS):
-                cols = slice(block * I, (block + 1) * I)
+            unit = step + BLOCK_LEAD - 1
+            if unit in range(BLOCKS):
+                m, rest = divmod(unit, PAIR_BLOCKS)
+                p, sj = divmod(rest, PAIR)
+                first = ((m * PAIR + sj) * K + p) * I
+                cols = slice(first, first + I)
                 nc.vector.quantize_mx(
-                    out=a_codes[:, cols].bitcast(E4M3_X4), scales=a_scales[:, cols], in_=a_grouped_of[block][:]
+                    out=a_codes[:, cols].bitcast(E4M3_X4),
+                    scales=a_scales[:, cols],
+                    in_=a_grouped_of[unit // 2][:, sj * I * PACK : (sj + 1) * I * PACK],
                 )
             if step in range(STEPS):
                 g_codes = codes_pool.tile([P, PAIR * P], U32, align_bytes=64)

@@ -31,6 +31,7 @@ BLOCK_LEAD = PAIRS * PAIR_BLOCKS - 1 - (PAIRS - 1) + 1
 TAIL_STEPS = 2
 BANK_SQUARES = 4
 STORE_LAG = 12
+FIRST_WARMERS = 6
 
 FLOPS = 2 * B * S * K * I * O
 BYTES = 2 * B * S * I + 2 * S * I * K * O + 2 * B * S * O + 4 * B * S * I
@@ -56,6 +57,16 @@ def tile_modelsingle_t_kernel(tc, x, taylor_a_0_1, taylor_a_0, grad_out, out):
         make_identity(nc, identity[:])
         a_codes = keep.tile([P, S * COLS], U32, align_bytes=64)
         a_scales = keep.tile([P, S * COLS], U8, align_bytes=64)
+
+        zeros = keep.tile([P, COLS], BF16)
+        nc.vector.memset(zeros[:], 0.0)
+
+        def warm():
+            acc = acc_psum.tile([P, COLS], F32)
+            nc.tensor.matmul(out=acc[:], lhsT=zeros[:, 0:P], rhs=zeros[:], start=True, stop=True)
+
+        for w in range(FIRST_WARMERS):
+            warm()
 
         a_raw_of = {}
         g_raw_of = {}
@@ -134,6 +145,8 @@ def tile_modelsingle_t_kernel(tc, x, taylor_a_0_1, taylor_a_0, grad_out, out):
                 flip_coefficients(step + BLOCK_LEAD)
             if step in range(STEPS):
                 flip_gradient(step)
+            elif step in range(-BLOCK_LEAD, 0):
+                warm()
 
         def quantise(step):
             unit = step + BLOCK_LEAD - 1

@@ -30,7 +30,7 @@ PAIR_BLOCKS = PAIR * K
 BLOCK_LEAD = PAIRS * PAIR_BLOCKS - 1 - (PAIRS - 1) + 1
 TAIL_STEPS = 2
 BANK_SQUARES = 4
-STORE_LAG = 12
+STORE_LAG = 22
 FIRST_WARMERS = 6
 
 FLOPS = 2 * B * S * K * I * O
@@ -48,7 +48,7 @@ def tile_modelsingle_t_kernel(tc, x, taylor_a_0_1, taylor_a_0, grad_out, out):
         grouped_pool = stack.enter_context(tc.tile_pool(name="grouped_pool", bufs=3))
         codes_pool = stack.enter_context(tc.tile_pool(name="codes_pool", bufs=3))
         work_pool = stack.enter_context(tc.tile_pool(name="work_pool", bufs=8))
-        out_pool = stack.enter_context(tc.tile_pool(name="out_pool", bufs=STORE_LAG // PAIRS + 3))
+        out_pool = stack.enter_context(tc.tile_pool(name="out_pool", bufs=STEPS // PAIRS))
         flipped_psum = stack.enter_context(tc.psum_pool(name="flipped_psum", bufs=4))
         acc_psum = stack.enter_context(tc.psum_pool(name="acc_psum", bufs=4))
         stack.enter_context(tc.manual_schedule())

from contextlib import ExitStack

import concourse.mybir as mybir
from concourse.masks import make_identity

F32 = mybir.dt.float32
BF16 = mybir.dt.bfloat16
U32 = mybir.dt.uint32
U8 = mybir.dt.uint8
E4M3_X4 = mybir.dt.float8_e4m3fn_x4
E5M2_X4 = mybir.dt.float8_e5m2_x4
MULT = mybir.AluOpType.mult
ADD = mybir.AluOpType.add

B, S, I, K, O = 512, 16, 256, 2, 512

P = 128
PACK = 4
HALVES = 2
B_TILES = B // P
I_PER_Q = 2 * I // P
COLS = K * I
PAIR = 2
GROUP = 8
PAIRS = GROUP // PAIR
GROUP_STEPS = B_TILES * PAIRS
STEPS = (S // GROUP) * GROUP_STEPS
BLOCKS = S * K
PAIR_BLOCKS = PAIR * K
BLOCK_LEAD = PAIRS * PAIR_BLOCKS - 1 - (PAIRS - 1) + 1
TAIL_STEPS = 2
BANK_SQUARES = 4
STORE_LAG = 22
FIRST_WARMERS = 6

FLOPS = 2 * B * S * K * I * O
BYTES = 2 * B * S * I + 2 * S * I * K * O + 2 * B * S * O + 4 * B * S * I


def tile_modelsingle_t_kernel(tc, x, taylor_a_0_1, taylor_a_0, grad_out, out):
    nc = tc.nc
    a_rows = taylor_a_0_1.rearrange("one (m sj) (q ih) p o -> (sj q) (one m) (ih p o)", sj=PAIR, ih=I_PER_Q)

    with ExitStack() as stack:
        keep = stack.enter_context(tc.tile_pool(name="keep", bufs=1))
        a_pool = stack.enter_context(tc.tile_pool(name="a_pool", bufs=4))
        gx_pool = stack.enter_context(tc.tile_pool(name="gx_pool", bufs=4))
        grouped_pool = stack.enter_context(tc.tile_pool(name="grouped_pool", bufs=3))
        codes_pool = stack.enter_context(tc.tile_pool(name="codes_pool", bufs=3))
        work_pool = stack.enter_context(tc.tile_pool(name="work_pool", bufs=8))
        out_pool = stack.enter_context(tc.tile_pool(name="out_pool", bufs=STEPS // PAIRS))
        flipped_psum = stack.enter_context(tc.psum_pool(name="flipped_psum", bufs=4))
        acc_psum = stack.enter_context(tc.psum_pool(name="acc_psum", bufs=4))
        stack.enter_context(tc.manual_schedule())

        identity = keep.tile([P, P], F32)
        make_identity(nc, identity[:])
        a_codes = keep.tile([P, S * COLS], U32, align_bytes=64)
        a_scales = keep.tile([P, S * COLS], U8, align_bytes=64)

        zeros = keep.tile([P, COLS], BF16)
        nc.vector.memset(zeros[:], 0.0)

        def warm():
            acc = acc_psum.tile([P, COLS], F32)
            nc.tensor.matmul(out=acc[:], lhsT=zeros[:, 0:P], rhs=zeros[:], start=True, stop=True)

        for w in range(FIRST_WARMERS):
            warm()

        a_raw_of = {}
        g_raw_of = {}
        x_of = {}
        a_grouped_of = {}
        g_grouped_of = {}
        g_mx_of = {}
        second_of = {}
        out_of = {}
        left_of = {}

        def where(step):
            group, rest = divmod(step, GROUP_STEPS)
            bt = rest // PAIRS
            return slice(bt * P, (bt + 1) * P), group * GROUP

        def load(step):
            block = step + BLOCK_LEAD
            if step in range(STEPS) and step % PAIRS == 0:
                b_rows, first = where(step)
                g_raw = gx_pool.tile([P, GROUP * O], BF16)
                nc.sync.dma_start(
                    out=g_raw[:], in_=grad_out[b_rows, first : first + GROUP, :].rearrange("b s o -> b (s o)")
                )
                g_raw_of[step // PAIRS] = g_raw
                x_sb = gx_pool.tile([P, GROUP * I], BF16)
                nc.sync.dma_start(
                    out=x_sb[:], in_=x[b_rows, first : first + GROUP, :].rearrange("b s i -> b (s i)")
                )
                x_of[step // PAIRS] = x_sb
            if block in range(BLOCKS) and block % PAIR_BLOCKS == 0:
                m = block // PAIR_BLOCKS
                a_raw = a_pool.tile([P, I_PER_Q * K * O], BF16)
                nc.sync.dma_start(out=a_raw[:], in_=a_rows[:, m : m + 1, :].rearrange("c m r -> c (m r)"))
                a_raw_of[m] = a_raw

        def flip_coefficients(block):
            p, h = divmod(block % PAIR_BLOCKS, 2)
            a_words = a_raw_of[block // PAIR_BLOCKS][:].bitcast(F32)
            a_flipped = flipped_psum.tile([P, BANK_SQUARES, P], F32, tag="flipped")
            for il in range(2):
                for u in range(HALVES):
                    first = (((2 * h + il) * K + p) * HALVES + u) * P
                    nc.tensor.transpose(
                        a_flipped[:, il * HALVES + u, :], a_words[:, first : first + P], identity[:]
                    )
            if h == 0:
                a_grouped = grouped_pool.tile([P, PAIR * I * PACK], BF16, align_bytes=64)
                a_grouped_of[block // 2] = a_grouped
            a_grouped = a_grouped_of[block // 2]
            nc.scalar.copy(
                out=a_grouped[:].bitcast(F32).rearrange("w (c r) -> w c r", r=2 * BANK_SQUARES)[
                    :, :, h * BANK_SQUARES : (h + 1) * BANK_SQUARES
                ],
                in_=a_flipped[:].rearrange("w r c -> w c r"),
            )

        def flip_gradient(step):
            g_words = g_raw_of[step // PAIRS][:].bitcast(F32)
            g_flipped = flipped_psum.tile([P, BANK_SQUARES, P], F32, tag="flipped")
            for j in range(PAIR):
                for u in range(HALVES):
                    first = (((step % PAIRS) * PAIR + j) * HALVES + u) * P
                    nc.tensor.transpose(
                        g_flipped[:, j * HALVES + u, :], g_words[:, first : first + P], identity[:]
                    )
            g_grouped = grouped_pool.tile([P, PAIR * P * PACK], BF16, align_bytes=64)
            nc.scalar.copy(
                out=g_grouped[:].bitcast(F32).rearrange("w (j b u) -> w j b u", j=PAIR, u=HALVES),
                in_=g_flipped[:].rearrange("w (j u) b -> w j b u", u=HALVES),
            )
            g_grouped_of[step] = g_grouped

        def flip(step):
            if step + BLOCK_LEAD in range(BLOCKS):
                flip_coefficients(step + BLOCK_LEAD)
            if step in range(STEPS):
                flip_gradient(step)
            elif step in range(-BLOCK_LEAD, 0):
                warm()

        def quantise(step):
            unit = step + BLOCK_LEAD - 1
            if unit in range(BLOCKS):
                m, rest = divmod(unit, PAIR_BLOCKS)
                p, sj = divmod(rest, PAIR)
                first = ((m * PAIR + sj) * K + p) * I
                cols = slice(first, first + I)
                nc.vector.quantize_mx(
                    out=a_codes[:, cols].bitcast(E4M3_X4),
                    scales=a_scales[:, cols],
                    in_=a_grouped_of[unit // 2][:, sj * I * PACK : (sj + 1) * I * PACK],
                )
            if step in range(STEPS):
                g_codes = codes_pool.tile([P, PAIR * P], U32, align_bytes=64)
                g_scales = codes_pool.tile([P, PAIR * P], U8, align_bytes=64)
                nc.vector.quantize_mx(
                    out=g_codes[:].bitcast(E5M2_X4), scales=g_scales[:], in_=g_grouped_of[step][:]
                )
                g_mx_of[step] = (g_codes, g_scales)

        def multiply(step):
            if step not in range(STEPS):
                return
            first = where(step)[1]
            g_codes, g_scales = g_mx_of[step]
            if step % PAIRS == 0:
                out_sb = out_pool.tile([P, GROUP * I], F32)
                out_of[step // PAIRS] = out_sb
            out_sb = out_of[step // PAIRS]
            accs = []
            for j in range(PAIR):
                s = first + (step % PAIRS) * PAIR + j
                acc = acc_psum.tile([P, COLS], F32)
                nc.tensor.matmul_mx(
                    out=acc[:],
                    lhsT=g_codes[:, j * P : (j + 1) * P].bitcast(E5M2_X4),
                    lhsT_scale=g_scales[:, j * P : (j + 1) * P],
                    rhs=a_codes[:, s * COLS : (s + 1) * COLS].bitcast(E4M3_X4),
                    rhs_scale=a_scales[:, s * COLS : (s + 1) * COLS],
                    start=True,
                    stop=True,
                )
                accs.append(acc)
            twice_x_h1s = []
            for j in range(PAIR):
                place = ((step % PAIRS) * PAIR + j) * I
                twice_x_h1 = work_pool.tile([P, I], F32)
                nc.vector.scalar_tensor_tensor(
                    out=twice_x_h1[:],
                    in0=accs[j][:, I : 2 * I],
                    scalar=2.0,
                    in1=x_of[step // PAIRS][:, place : place + I],
                    op0=MULT,
                    op1=MULT,
                )
                twice_x_h1s.append(twice_x_h1)
            place = (step % PAIRS) * PAIR * I
            left_of[step] = [] if step >= STEPS - TAIL_STEPS else [1]
            for j in range(PAIR):
                if j not in left_of[step]:
                    nc.vector.tensor_tensor(
                        out=out_sb[:, place + j * I : place + (j + 1) * I],
                        in0=twice_x_h1s[j][:],
                        in1=accs[j][:, 0:I],
                        op=ADD,
                    )
            second_of[step] = (accs, twice_x_h1s)

        def finish(step):
            if step not in range(STEPS):
                return
            accs, twice_x_h1s = second_of[step]
            for j in left_of[step]:
                place = ((step % PAIRS) * PAIR + j) * I
                result = out_of[step // PAIRS][:, place : place + I]
                nc.scalar.copy(out=result, in_=accs[j][:, 0:I])
                nc.gpsimd.tensor_tensor(out=result, in0=result, in1=twice_x_h1s[j][:], op=ADD)

        def store(step):
            if step not in range(STEPS):
                return
            b_rows, first = where(step)
            if step >= STEPS - PAIRS:
                k = step % PAIRS
                nc.sync.dma_start(
                    out=out[b_rows, first + k * PAIR : first + (k + 1) * PAIR, :].rearrange("b s i -> b (s i)"),
                    in_=out_of[step // PAIRS][:, k * PAIR * I : (k + 1) * PAIR * I],
                )
            elif step % PAIRS == PAIRS - 1:
                nc.sync.dma_start(
                    out=out[b_rows, first : first + GROUP, :].rearrange("b s i -> b (s i)"),
                    in_=out_of[step // PAIRS][:],
                )

        for n in range(-BLOCK_LEAD - 4, STEPS + STORE_LAG):
            load(n + 4)
            finish(n - 1)
            flip(n + 2)
            quantise(n + 1)
            multiply(n)
            store(n - STORE_LAG)
